import numpy as np
import ml_dtypes

BF16 = ml_dtypes.bfloat16


def bf(x):
    return np.asarray(x, np.float32).astype(BF16)


def f32(x):
    return np.asarray(x, np.float32)


def f64(x):
    return np.asarray(x).astype(np.float64)


def striped(idx):
    return np.tile(idx.reshape(-1, 16).T, (8, 1))


D, S, M, B, T, N = 128, 2048, 256, 256, 6, 1536
NEG_SLOPE = 0.2
MASK_VAL = -1e9
KEEP = 0.7


def setup_inputs():
    adj = (np.random.random((B, T, T)) < KEEP).astype(np.float32)
    adj[:, np.arange(T), np.arange(T)] = 1.0
    return {"table": bf(np.random.standard_normal((D, S))), "w": bf(np.random.standard_normal((D, M)) / np.sqrt(D)), "a_src": bf(np.random.standard_normal((M, 1)) / np.sqrt(2 * M)), "a_dst": bf(np.random.standard_normal((M, 1)) / np.sqrt(2 * M)), "adj": f32(adj.reshape(N, T)), "offs": striped(np.random.permutation(np.tile(np.arange(S), 2))[:N])}


def reference(table, w, a_src, a_dst, adj, offs):
    idx = offs[:16].T.reshape(-1)
    wh = f64(w).T @ f64(table)[:, idx]
    src = (f64(a_src).T @ wh).reshape(B, T, 1)
    dst = (f64(a_dst).T @ wh).reshape(B, 1, T)
    e = src + dst
    e = np.maximum(e, NEG_SLOPE * e)
    e = np.where(f64(adj).reshape(B, T, T) == 0.0, MASK_VAL, e)
    p = np.exp(e - e.max(axis=-1, keepdims=True))
    att = p / p.sum(axis=-1, keepdims=True)
    agg = np.einsum("bit,mbt->mbi", att, wh.reshape(M, B, T))
    return np.maximum(agg.reshape(M, N), 0.0)

@@ -1,0 +1,173 @@
+import concourse.mybir as mybir
+from concourse.masks import make_block_diagonal, make_identity
+
+BF16, F32, U16 = mybir.dt.bfloat16, mybir.dt.float32, mybir.dt.uint16
+ALU = mybir.AluOpType
+ACT = mybir.ActivationFunctionType
+X = mybir.AxisListType.X
+
+P = 128
+S = 2048
+M = 256
+N = 1536
+T = 6
+HALVES = M // P
+CHUNK = 96
+GRAPHS = CHUNK // T
+NCHUNK = N // CHUNK
+GROUP = 384
+CPG = GROUP // CHUNK
+NGROUP = N // GROUP
+NEG_SLOPE = 0.2
+MASK_VAL = -1e9
+
+FLOPS = 2 * N * M * (P + 2 + T)
+
+
+def tile_numbergraphencoder_kernel(tc, table, w, a_src, a_dst, adj, offs, out):
+    nc = tc.nc
+    with (
+        tc.tile_pool(name="held", bufs=1) as held,
+        tc.tile_pool(name="stage", bufs=3) as stage,
+        tc.psum_pool(name="psum", bufs=2) as psum,
+        tc.psum_pool(name="psum1", bufs=1) as psum1,
+    ):
+        offsets = held.tile([P, N // 16], U16, name="offsets")
+        nc.sync.dma_start(offsets[:], offs)
+        table_sb = held.tile([P, S], BF16, name="table_sb")
+        nc.sync.dma_start(table_sb[:], table)
+        w_sb = held.tile([P, M], BF16, name="w_sb")
+        nc.scalar.dma_start(w_sb[:], w)
+        a_rows = held.tile([2 * HALVES, P], BF16, name="a_rows")
+        nc.scalar.dma_start(a_rows[0:HALVES, :], a_src.rearrange("(h m) o -> h (m o)", h=HALVES))
+        nc.scalar.dma_start(a_rows[HALVES : 2 * HALVES, :], a_dst.rearrange("(h m) o -> h (m o)", h=HALVES))
+        adj_sb = held.tile([CHUNK, NCHUNK, T], F32, name="adj_sb")
+        nc.gpsimd.dma_start(adj_sb[:], adj.rearrange("(c p) t -> p c t", p=CHUNK))
+
+        ident = held.tile([P, P], F32, name="ident")
+        make_identity(nc, ident[:])
+        ident_bf = held.tile([2 * HALVES, 2 * HALVES], BF16, name="ident_bf")
+        make_identity(nc, ident_bf[:])
+        same_graph = held.tile([CHUNK, CHUNK], F32, name="same_graph")
+        make_block_diagonal(nc, same_graph[:], T)
+        node_onehot = held.tile([CHUNK, T], F32, name="node_onehot")
+        nc.vector.reduce_sum(node_onehot[:], ident[:CHUNK, :CHUNK].rearrange("p (g t) -> p t g", t=T), axis=X)
+        neg_fill = held.tile([CHUNK, NCHUNK, T], F32, name="neg_fill")
+        nc.vector.tensor_scalar(neg_fill[:], adj_sb[:], -1.0, -MASK_VAL, ALU.add, ALU.mult)
+
+        a_ps = psum1.tile([P, 2 * HALVES], BF16, name="a_ps", tag="small")
+        nc.tensor.transpose(a_ps[:], a_rows[:], ident_bf[:])
+        a_cols = held.tile([P, 2, HALVES], BF16, name="a_cols")
+        nc.vector.tensor_copy(a_cols[:].rearrange("p s h -> p (s h)"), a_ps[:])
+
+        wh_f32 = held.tile([P, HALVES, N], F32, name="wh_f32")
+        wh_bf = held.tile([P, HALVES, N], BF16, name="wh_bf")
+        for g in range(NGROUP):
+            cols = slice(g * GROUP, (g + 1) * GROUP)
+            piece = offsets[:, g * GROUP // 16 : (g + 1) * GROUP // 16]
+            for h in range(HALVES):
+                wh_ps = psum.tile([P, GROUP], F32, name="wh_ps")
+                nc.tensor.matmul(
+                    wh_ps[:], w_sb[:, h * P : (h + 1) * P], table_sb[:].indirect(piece), start=True, stop=True
+                )
+                if h == 0:
+                    nc.scalar.activation(wh_f32[:, h, cols], wh_ps[:], ACT.Copy)
+                else:
+                    nc.vector.tensor_copy(wh_f32[:, h, cols], wh_ps[:])
+                nc.gpsimd.tensor_copy(wh_bf[:, h, cols], wh_f32[:, h, cols])
+
+        sd_ps = psum1.tile([CHUNK, NCHUNK, 2], F32, name="sd_ps", tag="small")
+        for c in range(NCHUNK):
+            for h in range(HALVES):
+                nc.tensor.matmul(
+                    sd_ps[:, c, :],
+                    wh_bf[:, h, c * CHUNK : (c + 1) * CHUNK],
+                    a_cols[:, :, h],
+                    start=(h == 0),
+                    stop=(h == HALVES - 1),
+                )
+        sd = held.tile([CHUNK, NCHUNK, 2], F32, name="sd")
+        nc.vector.tensor_copy(sd[:], sd_ps[:])
+
+        whT = held.tile([CHUNK, NCHUNK, M], F32, name="whT")
+        for pair in range(NCHUNK // 2):
+            whT_ps = psum.tile([CHUNK, 2, M], F32, name="whT_ps")
+            for k in range(2):
+                c = 2 * pair + k
+                for h in range(HALVES):
+                    nc.tensor.transpose(
+                        whT_ps[:, k, h * P : (h + 1) * P], wh_f32[:, h, c * CHUNK : (c + 1) * CHUNK], ident[:]
+                    )
+            if pair % 2 == 0:
+                nc.scalar.activation(whT[:, 2 * pair : 2 * pair + 2, :], whT_ps[:], ACT.Copy)
+            else:
+                nc.vector.tensor_copy(whT[:, 2 * pair : 2 * pair + 2, :], whT_ps[:])
+
+        small = [CHUNK, NCHUNK, T]
+        dst_spread = held.tile(small, F32, name="dst_spread")
+        nc.vector.tensor_tensor(
+            dst_spread[:], sd[:, :, 1:2].to_broadcast(small), node_onehot[:].unsqueeze(1).to_broadcast(small), ALU.mult
+        )
+        dst_graph = psum1.tile(small, F32, name="dst_graph", tag="small")
+        nc.tensor.matmul(
+            dst_graph[:].rearrange("p c t -> p (c t)"),
+            same_graph[:],
+            dst_spread[:].rearrange("p c t -> p (c t)"),
+            start=True,
+            stop=True,
+        )
+        e = held.tile(small, F32, name="e")
+        nc.vector.tensor_tensor(e[:], dst_graph[:], sd[:, :, 0:1].to_broadcast(small), ALU.add)
+        nc.vector.scalar_tensor_tensor(e[:], e[:], NEG_SLOPE, e[:], ALU.mult, ALU.max)
+        nc.vector.tensor_tensor(e[:], e[:], adj_sb[:], ALU.mult)
+        nc.vector.tensor_tensor(e[:], e[:], neg_fill[:], ALU.add)
+        e_max = held.tile([CHUNK, NCHUNK], F32, name="e_max")
+        nc.vector.tensor_reduce(e_max[:], e[:], axis=X, op=ALU.max)
+        nc.vector.tensor_tensor(e[:], e[:], e_max[:].unsqueeze(2).to_broadcast(small), ALU.subtract)
+        att = held.tile(small, F32, name="att")
+        nc.scalar.activation(att[:], e[:], ACT.Exp)
+        att_sum = held.tile([CHUNK, NCHUNK], F32, name="att_sum")
+        nc.vector.tensor_reduce(att_sum[:], att[:], axis=X, op=ALU.add)
+        nc.vector.reciprocal(att_sum[:], att_sum[:])
+        nc.vector.tensor_tensor(att[:], att[:], att_sum[:].unsqueeze(2).to_broadcast(small), ALU.mult)
+
+        att_wide = held.tile([CHUNK, NCHUNK, GRAPHS, T], F32, name="att_wide")
+        attT = held.tile([CHUNK, NCHUNK, CHUNK], F32, name="attT")
+        wide = [CHUNK, CPG, GRAPHS, T]
+        for g in range(NGROUP):
+            chunks = slice(g * CPG, (g + 1) * CPG)
+            nc.vector.tensor_tensor(
+                att_wide[:, chunks],
+                att[:, chunks].unsqueeze(2).to_broadcast(wide),
+                same_graph[:].rearrange("p (g t) -> p g t", t=T).unsqueeze(1).to_broadcast(wide),
+                ALU.mult,
+            )
+            attT_ps = psum1.tile([CHUNK, CPG, CHUNK], F32, name="attT_ps")
+            for k in range(CPG):
+                nc.tensor.transpose(
+                    attT_ps[:, k, :],
+                    att_wide[:, g * CPG + k].rearrange("p g t -> p (g t)"),
+                    ident[:CHUNK, :CHUNK],
+                )
+            if g % 2 == 0:
+                nc.scalar.activation(attT[:, chunks, :], attT_ps[:], ACT.Copy)
+            else:
+                nc.vector.tensor_copy(attT[:, chunks, :], attT_ps[:])
+            for h in range(HALVES):
+                out_ps = psum.tile([P, GROUP], F32, name="out_ps")
+                for k in range(CPG):
+                    c = g * CPG + k
+                    nc.tensor.matmul(
+                        out_ps[:, k * CHUNK : (k + 1) * CHUNK],
+                        whT[:, c, h * P : (h + 1) * P],
+                        attT[:, c, :],
+                        start=True,
+                        stop=True,
+                    )
+                out_sb = stage.tile([P, GROUP], F32, name="out_sb")
+                if h == 0:
+                    nc.scalar.activation(out_sb[:], out_ps[:], ACT.Relu)
+                    nc.sync.dma_start(out[h * P : (h + 1) * P, g * GROUP : (g + 1) * GROUP], out_sb[:])
+                else:
+                    nc.vector.tensor_scalar_max(out_sb[:], out_ps[:], 0.0)
+                    nc.scalar.dma_start(out[h * P : (h + 1) * P, g * GROUP : (g + 1) * GROUP], out_sb[:])

@@ -11,7 +11,9 @@ S = 2048
 M = 256
 N = 1536
 T = 6
-HALVES = M // P
+BLOCKS = M // P
+BANK = 512
+PIECE = BANK
 CHUNK = 96
 GRAPHS = CHUNK // T
 NCHUNK = N // CHUNK
@@ -28,9 +30,10 @@ def tile_numbergraphencoder_kernel(tc, table, w, a_src, a_dst, adj, offs, out):
     nc = tc.nc
     with (
         tc.tile_pool(name="held", bufs=1) as held,
-        tc.tile_pool(name="stage", bufs=3) as stage,
-        tc.psum_pool(name="psum", bufs=2) as psum,
-        tc.psum_pool(name="psum1", bufs=1) as psum1,
+        tc.tile_pool(name="each", bufs=NGROUP) as each,
+        tc.tile_pool(name="stage", bufs=NGROUP * BLOCKS) as stage,
+        tc.psum_pool(name="banks", bufs=6) as banks,
+        tc.psum_pool(name="small_ps", bufs=2) as small_ps,
     ):
         offsets = held.tile([P, N // 16], U16, name="offsets")
         nc.sync.dma_start(offsets[:], offs)
@@ -38,15 +41,15 @@ def tile_numbergraphencoder_kernel(tc, table, w, a_src, a_dst, adj, offs, out):
         nc.sync.dma_start(table_sb[:], table)
         w_sb = held.tile([P, M], BF16, name="w_sb")
         nc.scalar.dma_start(w_sb[:], w)
-        a_rows = held.tile([2 * HALVES, P], BF16, name="a_rows")
-        nc.scalar.dma_start(a_rows[0:HALVES, :], a_src.rearrange("(h m) o -> h (m o)", h=HALVES))
-        nc.scalar.dma_start(a_rows[HALVES : 2 * HALVES, :], a_dst.rearrange("(h m) o -> h (m o)", h=HALVES))
+        a_rows = held.tile([2 * BLOCKS, P], BF16, name="a_rows")
+        nc.scalar.dma_start(a_rows[0:BLOCKS, :], a_src.rearrange("(b m) o -> b (m o)", b=BLOCKS))
+        nc.scalar.dma_start(a_rows[BLOCKS : 2 * BLOCKS, :], a_dst.rearrange("(b m) o -> b (m o)", b=BLOCKS))
         adj_sb = held.tile([CHUNK, NCHUNK, T], F32, name="adj_sb")
-        nc.gpsimd.dma_start(adj_sb[:], adj.rearrange("(c p) t -> p c t", p=CHUNK))
+        nc.sync.dma_start(adj_sb[:], adj.rearrange("(c p) t -> p c t", p=CHUNK))
 
         ident = held.tile([P, P], F32, name="ident")
         make_identity(nc, ident[:])
-        ident_bf = held.tile([2 * HALVES, 2 * HALVES], BF16, name="ident_bf")
+        ident_bf = held.tile([2 * BLOCKS, 2 * BLOCKS], BF16, name="ident_bf")
         make_identity(nc, ident_bf[:])
         same_graph = held.tile([CHUNK, CHUNK], F32, name="same_graph")
         make_block_diagonal(nc, same_graph[:], T)
@@ -54,61 +57,50 @@ def tile_numbergraphencoder_kernel(tc, table, w, a_src, a_dst, adj, offs, out):
         nc.vector.reduce_sum(node_onehot[:], ident[:CHUNK, :CHUNK].rearrange("p (g t) -> p t g", t=T), axis=X)
         neg_fill = held.tile([CHUNK, NCHUNK, T], F32, name="neg_fill")
         nc.vector.tensor_scalar(neg_fill[:], adj_sb[:], -1.0, -MASK_VAL, ALU.add, ALU.mult)
-
-        a_ps = psum1.tile([P, 2 * HALVES], BF16, name="a_ps", tag="small")
+        a_ps = small_ps.tile([P, 2 * BLOCKS], BF16, name="a_ps", tag="small")
         nc.tensor.transpose(a_ps[:], a_rows[:], ident_bf[:])
-        a_cols = held.tile([P, 2, HALVES], BF16, name="a_cols")
-        nc.vector.tensor_copy(a_cols[:].rearrange("p s h -> p (s h)"), a_ps[:])
+        a_cols = held.tile([P, 2, BLOCKS], BF16, name="a_cols")
+        nc.vector.tensor_copy(a_cols[:].rearrange("p s b -> p (s b)"), a_ps[:])
 
-        wh_f32 = held.tile([P, HALVES, N], F32, name="wh_f32")
-        wh_bf = held.tile([P, HALVES, N], BF16, name="wh_bf")
-        for g in range(NGROUP):
-            cols = slice(g * GROUP, (g + 1) * GROUP)
-            piece = offsets[:, g * GROUP // 16 : (g + 1) * GROUP // 16]
-            for h in range(HALVES):
-                wh_ps = psum.tile([P, GROUP], F32, name="wh_ps")
+        wh_f32 = held.tile([P, BLOCKS, N], F32, name="wh_f32")
+        wh_bf = held.tile([P, BLOCKS, N], BF16, name="wh_bf")
+        for i in range(N // PIECE):
+            cols = slice(i * PIECE, (i + 1) * PIECE)
+            piece = offsets[:, i * PIECE // 16 : (i + 1) * PIECE // 16]
+            for b in range(BLOCKS):
+                wh_ps = banks.tile([P, PIECE], F32, name="wh_ps", tag="bank")
                 nc.tensor.matmul(
-                    wh_ps[:], w_sb[:, h * P : (h + 1) * P], table_sb[:].indirect(piece), start=True, stop=True
+                    wh_ps[:], w_sb[:, b * P : (b + 1) * P], table_sb[:].indirect(piece), start=True, stop=True
                 )
-                if h == 0:
-                    nc.scalar.activation(wh_f32[:, h, cols], wh_ps[:], ACT.Copy)
+                if b == 0:
+                    nc.scalar.activation(wh_bf[:, b, cols], wh_ps[:], ACT.Copy)
+                    nc.scalar.activation(wh_f32[:, b, cols], wh_ps[:], ACT.Copy)
                 else:
-                    nc.vector.tensor_copy(wh_f32[:, h, cols], wh_ps[:])
-                nc.gpsimd.tensor_copy(wh_bf[:, h, cols], wh_f32[:, h, cols])
+                    nc.vector.tensor_copy(wh_bf[:, b, cols], wh_ps[:])
+                    nc.vector.tensor_copy(wh_f32[:, b, cols], wh_ps[:])
 
-        sd_ps = psum1.tile([CHUNK, NCHUNK, 2], F32, name="sd_ps", tag="small")
+        sd_ps = small_ps.tile([CHUNK, NCHUNK, 2], F32, name="sd_ps", tag="small")
         for c in range(NCHUNK):
-            for h in range(HALVES):
+            for b in range(BLOCKS):
                 nc.tensor.matmul(
                     sd_ps[:, c, :],
-                    wh_bf[:, h, c * CHUNK : (c + 1) * CHUNK],
-                    a_cols[:, :, h],
-                    start=(h == 0),
-                    stop=(h == HALVES - 1),
+                    wh_bf[:, b, c * CHUNK : (c + 1) * CHUNK],
+                    a_cols[:, :, b],
+                    start=(b == 0),
+                    stop=(b == BLOCKS - 1),
                 )
-        sd = held.tile([CHUNK, NCHUNK, 2], F32, name="sd")
-        nc.vector.tensor_copy(sd[:], sd_ps[:])
-
-        whT = held.tile([CHUNK, NCHUNK, M], F32, name="whT")
-        for pair in range(NCHUNK // 2):
-            whT_ps = psum.tile([CHUNK, 2, M], F32, name="whT_ps")
-            for k in range(2):
-                c = 2 * pair + k
-                for h in range(HALVES):
-                    nc.tensor.transpose(
-                        whT_ps[:, k, h * P : (h + 1) * P], wh_f32[:, h, c * CHUNK : (c + 1) * CHUNK], ident[:]
-                    )
-            if pair % 2 == 0:
-                nc.scalar.activation(whT[:, 2 * pair : 2 * pair + 2, :], whT_ps[:], ACT.Copy)
-            else:
-                nc.vector.tensor_copy(whT[:, 2 * pair : 2 * pair + 2, :], whT_ps[:])
 
         small = [CHUNK, NCHUNK, T]
         dst_spread = held.tile(small, F32, name="dst_spread")
         nc.vector.tensor_tensor(
-            dst_spread[:], sd[:, :, 1:2].to_broadcast(small), node_onehot[:].unsqueeze(1).to_broadcast(small), ALU.mult
+            dst_spread[:],
+            sd_ps[:, :, 1:2].to_broadcast(small),
+            node_onehot[:].unsqueeze(1).to_broadcast(small),
+            ALU.mult,
         )
-        dst_graph = psum1.tile(small, F32, name="dst_graph", tag="small")
+        src = held.tile([CHUNK, NCHUNK, 1], F32, name="src")
+        nc.vector.tensor_copy(src[:], sd_ps[:, :, 0:1])
+        dst_graph = small_ps.tile(small, F32, name="dst_graph", tag="small")
         nc.tensor.matmul(
             dst_graph[:].rearrange("p c t -> p (c t)"),
             same_graph[:],
@@ -117,7 +109,7 @@ def tile_numbergraphencoder_kernel(tc, table, w, a_src, a_dst, adj, offs, out):
             stop=True,
         )
         e = held.tile(small, F32, name="e")
-        nc.vector.tensor_tensor(e[:], dst_graph[:], sd[:, :, 0:1].to_broadcast(small), ALU.add)
+        nc.vector.tensor_tensor(e[:], dst_graph[:], src[:].to_broadcast(small), ALU.add)
         nc.vector.scalar_tensor_tensor(e[:], e[:], NEG_SLOPE, e[:], ALU.mult, ALU.max)
         nc.vector.tensor_tensor(e[:], e[:], adj_sb[:], ALU.mult)
         nc.vector.tensor_tensor(e[:], e[:], neg_fill[:], ALU.add)
@@ -131,43 +123,55 @@ def tile_numbergraphencoder_kernel(tc, table, w, a_src, a_dst, adj, offs, out):
         nc.vector.reciprocal(att_sum[:], att_sum[:])
         nc.vector.tensor_tensor(att[:], att[:], att_sum[:].unsqueeze(2).to_broadcast(small), ALU.mult)
 
-        att_wide = held.tile([CHUNK, NCHUNK, GRAPHS, T], F32, name="att_wide")
-        attT = held.tile([CHUNK, NCHUNK, CHUNK], F32, name="attT")
-        wide = [CHUNK, CPG, GRAPHS, T]
+        whT = []
         for g in range(NGROUP):
-            chunks = slice(g * CPG, (g + 1) * CPG)
+            whT.append(each.tile([CHUNK, CPG, M], F32, name="whT"))
+            for pair in range(CPG // 2):
+                whT_ps = banks.tile([CHUNK, 2, M], F32, name="whT_ps", tag="bank")
+                for k in range(2):
+                    first = g * GROUP + (2 * pair + k) * CHUNK
+                    for b in range(BLOCKS):
+                        nc.tensor.transpose(
+                            whT_ps[:, k, b * P : (b + 1) * P], wh_f32[:, b, first : first + CHUNK], ident[:]
+                        )
+                nc.scalar.activation(whT[g][:, 2 * pair : 2 * pair + 2, :], whT_ps[:], ACT.Copy)
+
+        wide = [CHUNK, CPG, GRAPHS, T]
+        attT = []
+
+        def attention_matrices(g):
+            att_wide = each.tile(wide, F32, name="att_wide")
             nc.vector.tensor_tensor(
-                att_wide[:, chunks],
-                att[:, chunks].unsqueeze(2).to_broadcast(wide),
+                att_wide[:],
+                att[:, g * CPG : (g + 1) * CPG].unsqueeze(2).to_broadcast(wide),
                 same_graph[:].rearrange("p (g t) -> p g t", t=T).unsqueeze(1).to_broadcast(wide),
                 ALU.mult,
             )
-            attT_ps = psum1.tile([CHUNK, CPG, CHUNK], F32, name="attT_ps")
-            for k in range(CPG):
+            attT_ps = banks.tile([CHUNK, CPG, CHUNK], F32, name="attT_ps", tag="bank")
+            for c in range(CPG):
                 nc.tensor.transpose(
-                    attT_ps[:, k, :],
-                    att_wide[:, g * CPG + k].rearrange("p g t -> p (g t)"),
-                    ident[:CHUNK, :CHUNK],
+                    attT_ps[:, c, :], att_wide[:, c].rearrange("p g t -> p (g t)"), ident[:CHUNK, :CHUNK]
                 )
-            if g % 2 == 0:
-                nc.scalar.activation(attT[:, chunks, :], attT_ps[:], ACT.Copy)
-            else:
-                nc.vector.tensor_copy(attT[:, chunks, :], attT_ps[:])
-            for h in range(HALVES):
-                out_ps = psum.tile([P, GROUP], F32, name="out_ps")
-                for k in range(CPG):
-                    c = g * CPG + k
+            attT.append(each.tile([CHUNK, CPG, CHUNK], F32, name="attT"))
+            nc.vector.tensor_copy(attT[g][:], attT_ps[:])
+
+        attention_matrices(0)
+        for g in range(NGROUP):
+            if g + 1 < NGROUP:
+                attention_matrices(g + 1)
+            for b in range(BLOCKS):
+                out_ps = banks.tile([P, GROUP], F32, name="out_ps", tag="bank")
+                for c in range(CPG):
                     nc.tensor.matmul(
-                        out_ps[:, k * CHUNK : (k + 1) * CHUNK],
-                        whT[:, c, h * P : (h + 1) * P],
-                        attT[:, c, :],
+                        out_ps[:, c * CHUNK : (c + 1) * CHUNK],
+                        whT[g][:, c, b * P : (b + 1) * P],
+                        attT[g][:, c, :],
                         start=True,
                         stop=True,
                     )
                 out_sb = stage.tile([P, GROUP], F32, name="out_sb")
-                if h == 0:
+                if b == 0:
                     nc.scalar.activation(out_sb[:], out_ps[:], ACT.Relu)
-                    nc.sync.dma_start(out[h * P : (h + 1) * P, g * GROUP : (g + 1) * GROUP], out_sb[:])
                 else:
                     nc.vector.tensor_scalar_max(out_sb[:], out_ps[:], 0.0)
-                    nc.scalar.dma_start(out[h * P : (h + 1) * P, g * GROUP : (g + 1) * GROUP], out_sb[:])
+                nc.sync.dma_start(out[b * P : (b + 1) * P, g * GROUP : (g + 1) * GROUP], out_sb[:])

@@ -20,6 +20,7 @@ NCHUNK = N // CHUNK
 GROUP = 384
 CPG = GROUP // CHUNK
 NGROUP = N // GROUP
+WARM = 8
 NEG_SLOPE = 0.2
 MASK_VAL = -1e9
 
@@ -46,6 +47,12 @@ def tile_numbergraphencoder_kernel(tc, table, w, a_src, a_dst, adj, offs, out):
         nc.scalar.dma_start(a_rows[BLOCKS : 2 * BLOCKS, :], a_dst.rearrange("(b m) o -> b (m o)", b=BLOCKS))
         adj_sb = held.tile([CHUNK, NCHUNK, T], F32, name="adj_sb")
         nc.sync.dma_start(adj_sb[:], adj.rearrange("(c p) t -> p c t", p=CHUNK))
+
+        zeros = held.tile([P, BANK], BF16, name="zeros")
+        nc.vector.memset(zeros[:], 0.0)
+        warm_ps = small_ps.tile([P, BANK], F32, name="warm_ps", tag="small")
+        for i in range(WARM):
+            nc.tensor.matmul(warm_ps[:], zeros[:, :P], zeros[:], start=True, stop=True)
 
         ident = held.tile([P, P], F32, name="ident")
         make_identity(nc, ident[:])

@@ -70,7 +70,8 @@ def tile_numbergraphencoder_kernel(tc, table, w, a_src, a_dst, adj, offs, out):
         nc.vector.tensor_copy(a_cols[:].rearrange("p s b -> p (s b)"), a_ps[:])
 
         wh_f32 = held.tile([P, BLOCKS, N], F32, name="wh_f32")
-        wh_bf = held.tile([P, BLOCKS, N], BF16, name="wh_bf")
+        wh_bf = held.tile([P, BLOCKS, N + P - CHUNK], BF16, name="wh_bf")
+        nc.vector.memset(wh_bf[:, :, N:], 0.0)
         for i in range(N // PIECE):
             cols = slice(i * PIECE, (i + 1) * PIECE)
             piece = offsets[:, i * PIECE // 16 : (i + 1) * PIECE // 16]
@@ -86,12 +87,12 @@ def tile_numbergraphencoder_kernel(tc, table, w, a_src, a_dst, adj, offs, out):
                     nc.vector.tensor_copy(wh_bf[:, b, cols], wh_ps[:])
                     nc.vector.tensor_copy(wh_f32[:, b, cols], wh_ps[:])
 
-        sd_ps = small_ps.tile([CHUNK, NCHUNK, 2], F32, name="sd_ps", tag="small")
+        sd_ps = small_ps.tile([P, NCHUNK, 2], F32, name="sd_ps", tag="small")
         for c in range(NCHUNK):
             for b in range(BLOCKS):
                 nc.tensor.matmul(
                     sd_ps[:, c, :],
-                    wh_bf[:, b, c * CHUNK : (c + 1) * CHUNK],
+                    wh_bf[:, b, c * CHUNK : c * CHUNK + P],
                     a_cols[:, :, b],
                     start=(b == 0),
                     stop=(b == BLOCKS - 1),
@@ -101,12 +102,12 @@ def tile_numbergraphencoder_kernel(tc, table, w, a_src, a_dst, adj, offs, out):
         dst_spread = held.tile(small, F32, name="dst_spread")
         nc.vector.tensor_tensor(
             dst_spread[:],
-            sd_ps[:, :, 1:2].to_broadcast(small),
+            sd_ps[:CHUNK, :, 1:2].to_broadcast(small),
             node_onehot[:].unsqueeze(1).to_broadcast(small),
             ALU.mult,
         )
         src = held.tile([CHUNK, NCHUNK, 1], F32, name="src")
-        nc.vector.tensor_copy(src[:], sd_ps[:, :, 0:1])
+        nc.vector.tensor_copy(src[:], sd_ps[:CHUNK, :, 0:1])
         dst_graph = small_ps.tile(small, F32, name="dst_graph", tag="small")
         nc.tensor.matmul(
             dst_graph[:].rearrange("p c t -> p (c t)"),
@@ -162,10 +163,9 @@ def tile_numbergraphencoder_kernel(tc, table, w, a_src, a_dst, adj, offs, out):
             attT.append(each.tile([CHUNK, CPG, CHUNK], F32, name="attT"))
             nc.vector.tensor_copy(attT[g][:], attT_ps[:])
 
-        attention_matrices(0)
         for g in range(NGROUP):
-            if g + 1 < NGROUP:
-                attention_matrices(g + 1)
+            attention_matrices(g)
+        for g in range(NGROUP):
             for b in range(BLOCKS):
                 out_ps = banks.tile([P, GROUP], F32, name="out_ps", tag="bank")
                 for c in range(CPG):
@@ -177,8 +177,5 @@ def tile_numbergraphencoder_kernel(tc, table, w, a_src, a_dst, adj, offs, out):
                         stop=True,
                     )
                 out_sb = stage.tile([P, GROUP], F32, name="out_sb")
-                if b == 0:
-                    nc.scalar.activation(out_sb[:], out_ps[:], ACT.Relu)
-                else:
-                    nc.vector.tensor_scalar_max(out_sb[:], out_ps[:], 0.0)
+                nc.scalar.activation(out_sb[:], out_ps[:], ACT.Relu)
                 nc.sync.dma_start(out[b * P : (b + 1) * P, g * GROUP : (g + 1) * GROUP], out_sb[:])

@@ -1,5 +1,5 @@
 import concourse.mybir as mybir
-from concourse.masks import make_block_diagonal, make_identity
+from concourse.masks import make_identity
 
 BF16, F32, U16 = mybir.dt.bfloat16, mybir.dt.float32, mybir.dt.uint16
 ALU = mybir.AluOpType
@@ -14,12 +14,14 @@ T = 6
 BLOCKS = M // P
 BANK = 512
 PIECE = BANK
+HALVES = N // T // P
 CHUNK = 96
 GRAPHS = CHUNK // T
-NCHUNK = N // CHUNK
+CPH = P // GRAPHS
 GROUP = 384
 CPG = GROUP // CHUNK
 NGROUP = N // GROUP
+PAIRS = T // 2
 WARM = 8
 NEG_SLOPE = 0.2
 MASK_VAL = -1e9
@@ -31,7 +33,8 @@ def tile_numbergraphencoder_kernel(tc, table, w, a_src, a_dst, adj, offs, out):
     nc = tc.nc
     with (
         tc.tile_pool(name="held", bufs=1) as held,
-        tc.tile_pool(name="each", bufs=NGROUP) as each,
+        tc.tile_pool(name="halves", bufs=HALVES) as halves,
+        tc.tile_pool(name="groups", bufs=NGROUP) as groups,
         tc.tile_pool(name="stage", bufs=NGROUP * BLOCKS) as stage,
         tc.psum_pool(name="banks", bufs=6) as banks,
         tc.psum_pool(name="small_ps", bufs=2) as small_ps,
@@ -45,8 +48,12 @@ def tile_numbergraphencoder_kernel(tc, table, w, a_src, a_dst, adj, offs, out):
         a_rows = held.tile([2 * BLOCKS, P], BF16, name="a_rows")
         nc.scalar.dma_start(a_rows[0:BLOCKS, :], a_src.rearrange("(b m) o -> b (m o)", b=BLOCKS))
         nc.scalar.dma_start(a_rows[BLOCKS : 2 * BLOCKS, :], a_dst.rearrange("(b m) o -> b (m o)", b=BLOCKS))
-        adj_sb = held.tile([CHUNK, NCHUNK, T], F32, name="adj_sb")
-        nc.sync.dma_start(adj_sb[:], adj.rearrange("(c p) t -> p c t", p=CHUNK))
+        small = [P, HALVES * T, T]
+        adj_sb = held.tile(small, F32, name="adj_sb")
+        nc.sync.dma_start(
+            adj_sb[:].rearrange("q (h i) t -> q h (i t)", h=HALVES),
+            adj.rearrange("(h q i) t -> q h (i t)", h=HALVES, i=T),
+        )
 
         zeros = held.tile([P, BANK], BF16, name="zeros")
         nc.vector.memset(zeros[:], 0.0)
@@ -58,11 +65,9 @@ def tile_numbergraphencoder_kernel(tc, table, w, a_src, a_dst, adj, offs, out):
         make_identity(nc, ident[:])
         ident_bf = held.tile([2 * BLOCKS, 2 * BLOCKS], BF16, name="ident_bf")
         make_identity(nc, ident_bf[:])
-        same_graph = held.tile([CHUNK, CHUNK], F32, name="same_graph")
-        make_block_diagonal(nc, same_graph[:], T)
-        node_onehot = held.tile([CHUNK, T], F32, name="node_onehot")
-        nc.vector.reduce_sum(node_onehot[:], ident[:CHUNK, :CHUNK].rearrange("p (g t) -> p t g", t=T), axis=X)
-        neg_fill = held.tile([CHUNK, NCHUNK, T], F32, name="neg_fill")
+        graph_onehot = held.tile([P, GRAPHS], F32, name="graph_onehot")
+        nc.vector.reduce_sum(graph_onehot[:], ident[:].rearrange("p (c g) -> p g c", g=GRAPHS), axis=X)
+        neg_fill = held.tile(small, F32, name="neg_fill")
         nc.vector.tensor_scalar(neg_fill[:], adj_sb[:], -1.0, -MASK_VAL, ALU.add, ALU.mult)
         a_ps = small_ps.tile([P, 2 * BLOCKS], BF16, name="a_ps", tag="small")
         nc.tensor.transpose(a_ps[:], a_rows[:], ident_bf[:])
@@ -70,8 +75,7 @@ def tile_numbergraphencoder_kernel(tc, table, w, a_src, a_dst, adj, offs, out):
         nc.vector.tensor_copy(a_cols[:].rearrange("p s b -> p (s b)"), a_ps[:])
 
         wh_f32 = held.tile([P, BLOCKS, N], F32, name="wh_f32")
-        wh_bf = held.tile([P, BLOCKS, N + P - CHUNK], BF16, name="wh_bf")
-        nc.vector.memset(wh_bf[:, :, N:], 0.0)
+        wh_bf = held.tile([P, BLOCKS, N], BF16, name="wh_bf")
         for i in range(N // PIECE):
             cols = slice(i * PIECE, (i + 1) * PIECE)
             piece = offsets[:, i * PIECE // 16 : (i + 1) * PIECE // 16]
@@ -87,53 +91,46 @@ def tile_numbergraphencoder_kernel(tc, table, w, a_src, a_dst, adj, offs, out):
                     nc.vector.tensor_copy(wh_bf[:, b, cols], wh_ps[:])
                     nc.vector.tensor_copy(wh_f32[:, b, cols], wh_ps[:])
 
-        sd_ps = small_ps.tile([P, NCHUNK, 2], F32, name="sd_ps", tag="small")
-        for c in range(NCHUNK):
-            for b in range(BLOCKS):
-                nc.tensor.matmul(
-                    sd_ps[:, c, :],
-                    wh_bf[:, b, c * CHUNK : c * CHUNK + P],
-                    a_cols[:, :, b],
-                    start=(b == 0),
-                    stop=(b == BLOCKS - 1),
-                )
+        by_node = wh_bf[:].rearrange("m b (q i) -> m b i q", i=T)
+        sd_ps = small_ps.tile([P, HALVES * T, 2], F32, name="sd_ps", tag="small")
+        for h in range(HALVES):
+            for i in range(T):
+                for b in range(BLOCKS):
+                    nc.tensor.matmul(
+                        sd_ps[:, h * T + i, :],
+                        by_node[:, b, i, h * P : (h + 1) * P],
+                        a_cols[:, :, b],
+                        start=(b == 0),
+                        stop=(b == BLOCKS - 1),
+                    )
 
-        small = [CHUNK, NCHUNK, T]
-        dst_spread = held.tile(small, F32, name="dst_spread")
-        nc.vector.tensor_tensor(
-            dst_spread[:],
-            sd_ps[:CHUNK, :, 1:2].to_broadcast(small),
-            node_onehot[:].unsqueeze(1).to_broadcast(small),
-            ALU.mult,
-        )
-        src = held.tile([CHUNK, NCHUNK, 1], F32, name="src")
-        nc.vector.tensor_copy(src[:], sd_ps[:CHUNK, :, 0:1])
-        dst_graph = small_ps.tile(small, F32, name="dst_graph", tag="small")
-        nc.tensor.matmul(
-            dst_graph[:].rearrange("p c t -> p (c t)"),
-            same_graph[:],
-            dst_spread[:].rearrange("p c t -> p (c t)"),
-            start=True,
-            stop=True,
-        )
+        sd = held.tile([P, HALVES * T, 2], F32, name="sd")
+        nc.vector.tensor_copy(sd[:], sd_ps[:])
+        by_half = [P, HALVES, T, T]
         e = held.tile(small, F32, name="e")
-        nc.vector.tensor_tensor(e[:], dst_graph[:], src[:].to_broadcast(small), ALU.add)
+        sd_by_half = sd[:].rearrange("q (h i) s -> q h i s", h=HALVES)
+        nc.vector.tensor_tensor(
+            e[:].rearrange("q (h i) t -> q h i t", h=HALVES),
+            sd_by_half[:, :, :, 0:1].to_broadcast(by_half),
+            sd_by_half[:, :, :, 1].unsqueeze(2).to_broadcast(by_half),
+            ALU.add,
+        )
         nc.vector.scalar_tensor_tensor(e[:], e[:], NEG_SLOPE, e[:], ALU.mult, ALU.max)
         nc.vector.tensor_tensor(e[:], e[:], adj_sb[:], ALU.mult)
         nc.vector.tensor_tensor(e[:], e[:], neg_fill[:], ALU.add)
-        e_max = held.tile([CHUNK, NCHUNK], F32, name="e_max")
+        e_max = held.tile([P, HALVES * T], F32, name="e_max")
         nc.vector.tensor_reduce(e_max[:], e[:], axis=X, op=ALU.max)
         nc.vector.tensor_tensor(e[:], e[:], e_max[:].unsqueeze(2).to_broadcast(small), ALU.subtract)
         att = held.tile(small, F32, name="att")
         nc.scalar.activation(att[:], e[:], ACT.Exp)
-        att_sum = held.tile([CHUNK, NCHUNK], F32, name="att_sum")
+        att_sum = held.tile([P, HALVES * T], F32, name="att_sum")
         nc.vector.tensor_reduce(att_sum[:], att[:], axis=X, op=ALU.add)
         nc.vector.reciprocal(att_sum[:], att_sum[:])
         nc.vector.tensor_tensor(att[:], att[:], att_sum[:].unsqueeze(2).to_broadcast(small), ALU.mult)
 
         whT = []
         for g in range(NGROUP):
-            whT.append(each.tile([CHUNK, CPG, M], F32, name="whT"))
+            whT.append(groups.tile([CHUNK, CPG, M], F32, name="whT"))
             for pair in range(CPG // 2):
                 whT_ps = banks.tile([CHUNK, 2, M], F32, name="whT_ps", tag="bank")
                 for k in range(2):
@@ -144,38 +141,39 @@ def tile_numbergraphencoder_kernel(tc, table, w, a_src, a_dst, adj, offs, out):
                         )
                 nc.scalar.activation(whT[g][:, 2 * pair : 2 * pair + 2, :], whT_ps[:], ACT.Copy)
 
-        wide = [CHUNK, CPG, GRAPHS, T]
+        wide = [P, T, GRAPHS, T]
         attT = []
-
-        def attention_matrices(g):
-            att_wide = each.tile(wide, F32, name="att_wide")
+        for h in range(HALVES):
+            att_wide = halves.tile(wide, F32, name="att_wide")
             nc.vector.tensor_tensor(
                 att_wide[:],
-                att[:, g * CPG : (g + 1) * CPG].unsqueeze(2).to_broadcast(wide),
-                same_graph[:].rearrange("p (g t) -> p g t", t=T).unsqueeze(1).to_broadcast(wide),
+                att[:, h * T : (h + 1) * T, :].unsqueeze(2).to_broadcast(wide),
+                graph_onehot[:].unsqueeze(1).unsqueeze(3).to_broadcast(wide),
                 ALU.mult,
             )
-            attT_ps = banks.tile([CHUNK, CPG, CHUNK], F32, name="attT_ps", tag="bank")
-            for c in range(CPG):
-                nc.tensor.transpose(
-                    attT_ps[:, c, :], att_wide[:, c].rearrange("p g t -> p (g t)"), ident[:CHUNK, :CHUNK]
-                )
-            attT.append(each.tile([CHUNK, CPG, CHUNK], F32, name="attT"))
-            nc.vector.tensor_copy(attT[g][:], attT_ps[:])
+            attT.append(halves.tile([CHUNK, PAIRS, P, 2], F32, name="attT"))
+            for a in range(PAIRS):
+                attT_ps = banks.tile([CHUNK, P, 2], F32, name="attT_ps", tag="bank")
+                for l in range(2):
+                    nc.tensor.transpose(
+                        attT_ps[:, :, l], att_wide[:, 2 * a + l].rearrange("q g t -> q (g t)"), ident[:]
+                    )
+                nc.vector.tensor_copy(attT[h][:, a], attT_ps[:])
 
         for g in range(NGROUP):
-            attention_matrices(g)
-        for g in range(NGROUP):
             for b in range(BLOCKS):
-                out_ps = banks.tile([P, GROUP], F32, name="out_ps", tag="bank")
-                for c in range(CPG):
+                out_ps = banks.tile([P, PAIRS, CPG * GRAPHS, 2], F32, name="out_ps", tag="bank")
+                for k in range(CPG):
+                    h, c = divmod(g * CPG + k, CPH)
                     nc.tensor.matmul(
-                        out_ps[:, c * CHUNK : (c + 1) * CHUNK],
-                        whT[g][:, c, b * P : (b + 1) * P],
-                        attT[g][:, c, :],
+                        out_ps[:, :, k * GRAPHS : (k + 1) * GRAPHS, :],
+                        whT[g][:, k, b * P : (b + 1) * P],
+                        attT[h][:, :, c * GRAPHS : (c + 1) * GRAPHS, :],
                         start=True,
                         stop=True,
                     )
-                out_sb = stage.tile([P, GROUP], F32, name="out_sb")
-                nc.scalar.activation(out_sb[:], out_ps[:], ACT.Relu)
-                nc.sync.dma_start(out[b * P : (b + 1) * P, g * GROUP : (g + 1) * GROUP], out_sb[:])
+                out_sb = stage.tile([P, CPG * GRAPHS, PAIRS, 2], F32, name="out_sb")
+                nc.scalar.activation(out_sb[:], out_ps[:].rearrange("m a q l -> m q a l"), ACT.Relu)
+                nc.sync.dma_start(
+                    out[b * P : (b + 1) * P, g * GROUP : (g + 1) * GROUP], out_sb[:].rearrange("m q a l -> m (q a l)")
+                )

@@ -25,6 +25,7 @@ PAIRS = T // 2
 WARM = 8
 NEG_SLOPE = 0.2
 MASK_VAL = -1e9
+HUGE = 3e38
 
 FLOPS = 2 * N * M * (P + 2 + T)
 
@@ -48,8 +49,7 @@ def tile_numbergraphencoder_kernel(tc, table, w, a_src, a_dst, adj, offs, out):
         a_rows = held.tile([2 * BLOCKS, P], BF16, name="a_rows")
         nc.scalar.dma_start(a_rows[0:BLOCKS, :], a_src.rearrange("(b m) o -> b (m o)", b=BLOCKS))
         nc.scalar.dma_start(a_rows[BLOCKS : 2 * BLOCKS, :], a_dst.rearrange("(b m) o -> b (m o)", b=BLOCKS))
-        small = [P, HALVES * T, T]
-        adj_sb = held.tile(small, F32, name="adj_sb")
+        adj_sb = held.tile([P, HALVES * T, T], F32, name="adj_sb")
         nc.sync.dma_start(
             adj_sb[:].rearrange("q (h i) t -> q h (i t)", h=HALVES),
             adj.rearrange("(h q i) t -> q h (i t)", h=HALVES, i=T),
@@ -67,8 +67,8 @@ def tile_numbergraphencoder_kernel(tc, table, w, a_src, a_dst, adj, offs, out):
         make_identity(nc, ident_bf[:])
         graph_onehot = held.tile([P, GRAPHS], F32, name="graph_onehot")
         nc.vector.reduce_sum(graph_onehot[:], ident[:].rearrange("p (c g) -> p g c", g=GRAPHS), axis=X)
-        neg_fill = held.tile(small, F32, name="neg_fill")
-        nc.vector.tensor_scalar(neg_fill[:], adj_sb[:], -1.0, -MASK_VAL, ALU.add, ALU.mult)
+        cap = held.tile([P, HALVES * T, T], F32, name="cap")
+        nc.vector.tensor_scalar(cap[:], adj_sb[:], HUGE, MASK_VAL, ALU.mult, ALU.add)
         a_ps = small_ps.tile([P, 2 * BLOCKS], BF16, name="a_ps", tag="small")
         nc.tensor.transpose(a_ps[:], a_rows[:], ident_bf[:])
         a_cols = held.tile([P, 2, BLOCKS], BF16, name="a_cols")
@@ -92,41 +92,40 @@ def tile_numbergraphencoder_kernel(tc, table, w, a_src, a_dst, adj, offs, out):
                     nc.vector.tensor_copy(wh_f32[:, b, cols], wh_ps[:])
 
         by_node = wh_bf[:].rearrange("m b (q i) -> m b i q", i=T)
-        sd_ps = small_ps.tile([P, HALVES * T, 2], F32, name="sd_ps", tag="small")
+        sd_ps = []
         for h in range(HALVES):
+            sd_ps.append(small_ps.tile([P, T, 2], F32, name="sd_ps", tag="small"))
             for i in range(T):
                 for b in range(BLOCKS):
                     nc.tensor.matmul(
-                        sd_ps[:, h * T + i, :],
+                        sd_ps[h][:, i, :],
                         by_node[:, b, i, h * P : (h + 1) * P],
                         a_cols[:, :, b],
                         start=(b == 0),
                         stop=(b == BLOCKS - 1),
                     )
 
-        sd = held.tile([P, HALVES * T, 2], F32, name="sd")
-        nc.vector.tensor_copy(sd[:], sd_ps[:])
-        by_half = [P, HALVES, T, T]
-        e = held.tile(small, F32, name="e")
-        sd_by_half = sd[:].rearrange("q (h i) s -> q h i s", h=HALVES)
-        nc.vector.tensor_tensor(
-            e[:].rearrange("q (h i) t -> q h i t", h=HALVES),
-            sd_by_half[:, :, :, 0:1].to_broadcast(by_half),
-            sd_by_half[:, :, :, 1].unsqueeze(2).to_broadcast(by_half),
-            ALU.add,
-        )
-        nc.vector.scalar_tensor_tensor(e[:], e[:], NEG_SLOPE, e[:], ALU.mult, ALU.max)
-        nc.vector.tensor_tensor(e[:], e[:], adj_sb[:], ALU.mult)
-        nc.vector.tensor_tensor(e[:], e[:], neg_fill[:], ALU.add)
-        e_max = held.tile([P, HALVES * T], F32, name="e_max")
-        nc.vector.tensor_reduce(e_max[:], e[:], axis=X, op=ALU.max)
-        nc.vector.tensor_tensor(e[:], e[:], e_max[:].unsqueeze(2).to_broadcast(small), ALU.subtract)
-        att = held.tile(small, F32, name="att")
-        nc.scalar.activation(att[:], e[:], ACT.Exp)
-        att_sum = held.tile([P, HALVES * T], F32, name="att_sum")
-        nc.vector.tensor_reduce(att_sum[:], att[:], axis=X, op=ALU.add)
-        nc.vector.reciprocal(att_sum[:], att_sum[:])
-        nc.vector.tensor_tensor(att[:], att[:], att_sum[:].unsqueeze(2).to_broadcast(small), ALU.mult)
+        small = [P, T, T]
+        att = []
+        for h in range(HALVES):
+            of_half = slice(h * T, (h + 1) * T)
+            sd = halves.tile([P, T, 2], F32, name="sd")
+            nc.vector.tensor_copy(sd[:], sd_ps[h][:])
+            e = halves.tile(small, F32, name="e")
+            nc.vector.tensor_tensor(
+                e[:], sd[:, :, 0:1].to_broadcast(small), sd[:, :, 1].unsqueeze(1).to_broadcast(small), ALU.add
+            )
+            nc.vector.scalar_tensor_tensor(e[:], e[:], NEG_SLOPE, e[:], ALU.mult, ALU.max)
+            nc.vector.tensor_tensor(e[:], e[:], cap[:, of_half], ALU.min)
+            e_max = halves.tile([P, T], F32, name="e_max")
+            nc.vector.tensor_reduce(e_max[:], e[:], axis=X, op=ALU.max)
+            nc.vector.tensor_tensor(e[:], e[:], e_max[:].unsqueeze(2).to_broadcast(small), ALU.subtract)
+            att.append(halves.tile(small, F32, name="att"))
+            nc.scalar.activation(att[h][:], e[:], ACT.Exp)
+            att_sum = halves.tile([P, T], F32, name="att_sum")
+            nc.vector.tensor_reduce(att_sum[:], att[h][:], axis=X, op=ALU.add)
+            nc.vector.reciprocal(att_sum[:], att_sum[:])
+            nc.vector.tensor_tensor(att[h][:], att[h][:], att_sum[:].unsqueeze(2).to_broadcast(small), ALU.mult)
 
         whT = []
         for g in range(NGROUP):
@@ -147,7 +146,7 @@ def tile_numbergraphencoder_kernel(tc, table, w, a_src, a_dst, adj, offs, out):
             att_wide = halves.tile(wide, F32, name="att_wide")
             nc.vector.tensor_tensor(
                 att_wide[:],
-                att[:, h * T : (h + 1) * T, :].unsqueeze(2).to_broadcast(wide),
+                att[h][:].unsqueeze(2).to_broadcast(wide),
                 graph_onehot[:].unsqueeze(1).unsqueeze(3).to_broadcast(wide),
                 ALU.mult,
             )

@@ -25,6 +25,7 @@ PAIRS = T // 2
 WARM = 8
 NEG_SLOPE = 0.2
 MASK_VAL = -1e9
+A_STEP = 16
 HUGE = 3e38
 
 FLOPS = 2 * N * M * (P + 2 + T)
@@ -46,9 +47,9 @@ def tile_numbergraphencoder_kernel(tc, table, w, a_src, a_dst, adj, offs, out):
         nc.sync.dma_start(table_sb[:], table)
         w_sb = held.tile([P, M], BF16, name="w_sb")
         nc.scalar.dma_start(w_sb[:], w)
-        a_rows = held.tile([2 * BLOCKS, P], BF16, name="a_rows")
-        nc.scalar.dma_start(a_rows[0:BLOCKS, :], a_src.rearrange("(b m) o -> b (m o)", b=BLOCKS))
-        nc.scalar.dma_start(a_rows[BLOCKS : 2 * BLOCKS, :], a_dst.rearrange("(b m) o -> b (m o)", b=BLOCKS))
+        a_cols = held.tile([P, 2, A_STEP], BF16, name="a_cols")
+        nc.scalar.dma_start(a_cols[:, 0, 0:BLOCKS], a_src.rearrange("(m b) o -> m (b o)", b=BLOCKS))
+        nc.scalar.dma_start(a_cols[:, 1, 0:BLOCKS], a_dst.rearrange("(m b) o -> m (b o)", b=BLOCKS))
         adj_sb = held.tile([P, HALVES * T, T], F32, name="adj_sb")
         nc.sync.dma_start(
             adj_sb[:].rearrange("q (h i) t -> q h (i t)", h=HALVES),
@@ -63,17 +64,12 @@ def tile_numbergraphencoder_kernel(tc, table, w, a_src, a_dst, adj, offs, out):
 
         ident = held.tile([P, P], F32, name="ident")
         make_identity(nc, ident[:])
-        ident_bf = held.tile([2 * BLOCKS, 2 * BLOCKS], BF16, name="ident_bf")
-        make_identity(nc, ident_bf[:])
         graph_onehot = held.tile([P, GRAPHS], F32, name="graph_onehot")
         nc.vector.reduce_sum(graph_onehot[:], ident[:].rearrange("p (c g) -> p g c", g=GRAPHS), axis=X)
         cap = held.tile([P, HALVES * T, T], F32, name="cap")
         nc.vector.tensor_scalar(cap[:], adj_sb[:], HUGE, MASK_VAL, ALU.mult, ALU.add)
-        a_ps = small_ps.tile([P, 2 * BLOCKS], BF16, name="a_ps", tag="small")
-        nc.tensor.transpose(a_ps[:], a_rows[:], ident_bf[:])
-        a_cols = held.tile([P, 2, BLOCKS], BF16, name="a_cols")
-        nc.vector.tensor_copy(a_cols[:].rearrange("p s b -> p (s b)"), a_ps[:])
 
+        w_block = w_sb[:].rearrange("k (m b) -> k b m", b=BLOCKS)
         wh_f32 = held.tile([P, BLOCKS, N], F32, name="wh_f32")
         wh_bf = held.tile([P, BLOCKS, N], BF16, name="wh_bf")
         for i in range(N // PIECE):
@@ -82,7 +78,7 @@ def tile_numbergraphencoder_kernel(tc, table, w, a_src, a_dst, adj, offs, out):
             for b in range(BLOCKS):
                 wh_ps = banks.tile([P, PIECE], F32, name="wh_ps", tag="bank")
                 nc.tensor.matmul(
-                    wh_ps[:], w_sb[:, b * P : (b + 1) * P], table_sb[:].indirect(piece), start=True, stop=True
+                    wh_ps[:], w_block[:, b], table_sb[:].indirect(piece), start=True, stop=True
                 )
                 if b == 0:
                     nc.scalar.activation(wh_bf[:, b, cols], wh_ps[:], ACT.Copy)
@@ -159,6 +155,7 @@ def tile_numbergraphencoder_kernel(tc, table, w, a_src, a_dst, adj, offs, out):
                     )
                 nc.vector.tensor_copy(attT[h][:, a], attT_ps[:])
 
+        out_block = out.rearrange("(m b) j -> b m j", b=BLOCKS)
         for g in range(NGROUP):
             for b in range(BLOCKS):
                 out_ps = banks.tile([P, PAIRS, CPG * GRAPHS, 2], F32, name="out_ps", tag="bank")
@@ -174,5 +171,5 @@ def tile_numbergraphencoder_kernel(tc, table, w, a_src, a_dst, adj, offs, out):
                 out_sb = stage.tile([P, CPG * GRAPHS, PAIRS, 2], F32, name="out_sb")
                 nc.scalar.activation(out_sb[:], out_ps[:].rearrange("m a q l -> m q a l"), ACT.Relu)
                 nc.sync.dma_start(
-                    out[b * P : (b + 1) * P, g * GROUP : (g + 1) * GROUP], out_sb[:].rearrange("m q a l -> m (q a l)")
+                    out_block[b, :, g * GROUP : (g + 1) * GROUP], out_sb[:].rearrange("m q a l -> m (q a l)")
                 )

@@ -13,11 +13,11 @@ N = 1536
 T = 6
 BLOCKS = M // P
 BANK = 512
-PIECE = BANK
 HALVES = N // T // P
 CHUNK = 96
 GRAPHS = CHUNK // T
 CPH = P // GRAPHS
+PIECE = BANK
 GROUP = 384
 CPG = GROUP // CHUNK
 NGROUP = N // GROUP
@@ -25,8 +25,8 @@ PAIRS = T // 2
 WARM = 8
 NEG_SLOPE = 0.2
 MASK_VAL = -1e9
-A_STEP = 16
 HUGE = 3e38
+A_STEP = 16
 
 FLOPS = 2 * N * M * (P + 2 + T)
 
@@ -64,22 +64,26 @@ def tile_numbergraphencoder_kernel(tc, table, w, a_src, a_dst, adj, offs, out):
 
         ident = held.tile([P, P], F32, name="ident")
         make_identity(nc, ident[:])
-        graph_onehot = held.tile([P, GRAPHS], F32, name="graph_onehot")
-        nc.vector.reduce_sum(graph_onehot[:], ident[:].rearrange("p (c g) -> p g c", g=GRAPHS), axis=X)
         cap = held.tile([P, HALVES * T, T], F32, name="cap")
-        nc.vector.tensor_scalar(cap[:], adj_sb[:], HUGE, MASK_VAL, ALU.mult, ALU.add)
+        nc.vector.tensor_scalar(cap[:], adj_sb[:], HUGE, MASK_VAL / NEG_SLOPE, ALU.mult, ALU.add)
+        own_graph = held.tile([CHUNK, GRAPHS], F32, name="own_graph")
+        nc.gpsimd.memset(own_graph[:], 1.0)
+        nc.gpsimd.affine_select(
+            own_graph[:], own_graph[:], [[-T, GRAPHS]], ALU.is_ge, 0.0, base=0, channel_multiplier=1
+        )
+        nc.gpsimd.affine_select(
+            own_graph[:], own_graph[:], [[T, GRAPHS]], ALU.is_ge, 0.0, base=T - 1, channel_multiplier=-1
+        )
 
         w_block = w_sb[:].rearrange("k (m b) -> k b m", b=BLOCKS)
-        wh_f32 = held.tile([P, BLOCKS, N], F32, name="wh_f32")
         wh_bf = held.tile([P, BLOCKS, N], BF16, name="wh_bf")
+        wh_f32 = held.tile([P, BLOCKS, N], F32, name="wh_f32")
         for i in range(N // PIECE):
             cols = slice(i * PIECE, (i + 1) * PIECE)
             piece = offsets[:, i * PIECE // 16 : (i + 1) * PIECE // 16]
             for b in range(BLOCKS):
                 wh_ps = banks.tile([P, PIECE], F32, name="wh_ps", tag="bank")
-                nc.tensor.matmul(
-                    wh_ps[:], w_block[:, b], table_sb[:].indirect(piece), start=True, stop=True
-                )
+                nc.tensor.matmul(wh_ps[:], w_block[:, b], table_sb[:].indirect(piece), start=True, stop=True)
                 if b == 0:
                     nc.scalar.activation(wh_bf[:, b, cols], wh_ps[:], ACT.Copy)
                     nc.scalar.activation(wh_f32[:, b, cols], wh_ps[:], ACT.Copy)
@@ -87,45 +91,36 @@ def tile_numbergraphencoder_kernel(tc, table, w, a_src, a_dst, adj, offs, out):
                     nc.vector.tensor_copy(wh_bf[:, b, cols], wh_ps[:])
                     nc.vector.tensor_copy(wh_f32[:, b, cols], wh_ps[:])
 
-        by_node = wh_bf[:].rearrange("m b (q i) -> m b i q", i=T)
-        sd_ps = []
-        for h in range(HALVES):
-            sd_ps.append(small_ps.tile([P, T, 2], F32, name="sd_ps", tag="small"))
-            for i in range(T):
-                for b in range(BLOCKS):
-                    nc.tensor.matmul(
-                        sd_ps[h][:, i, :],
-                        by_node[:, b, i, h * P : (h + 1) * P],
-                        a_cols[:, :, b],
-                        start=(b == 0),
-                        stop=(b == BLOCKS - 1),
-                    )
-
         small = [P, T, T]
-        att = []
-        for h in range(HALVES):
-            of_half = slice(h * T, (h + 1) * T)
-            sd = halves.tile([P, T, 2], F32, name="sd")
-            nc.vector.tensor_copy(sd[:], sd_ps[h][:])
+        att = [halves.tile(small, F32, name="att") for h in range(HALVES)]
+        inv_sum = [halves.tile([P, T], F32, name="inv_sum") for h in range(HALVES)]
+
+        by_node = wh_bf[:].rearrange("m b (q n) -> m b n q", n=T)
+
+        def softmax(h):
+            of_half = slice(h * P, (h + 1) * P)
+            e_ps = small_ps.tile(small, F32, name="e_ps", tag="small")
+            for b in reversed(range(BLOCKS)):
+                a_row, a_col = (a_cols[:, s, b : b + 1].to_broadcast([P, T]) for s in range(2))
+                for n in range(T):
+                    first = b == BLOCKS - 1 and n == 0
+                    nc.tensor.matmul(e_ps[:, n], by_node[:, b, n, of_half], a_row, start=first, stop=False)
+                for n in range(T):
+                    last = b == 0 and n == T - 1
+                    nc.tensor.matmul(e_ps[:, :, n], by_node[:, b, n, of_half], a_col, start=False, stop=last)
             e = halves.tile(small, F32, name="e")
-            nc.vector.tensor_tensor(
-                e[:], sd[:, :, 0:1].to_broadcast(small), sd[:, :, 1].unsqueeze(1).to_broadcast(small), ALU.add
-            )
+            nc.vector.tensor_tensor(e[:], e_ps[:], cap[:, h * T : (h + 1) * T], ALU.min)
             nc.vector.scalar_tensor_tensor(e[:], e[:], NEG_SLOPE, e[:], ALU.mult, ALU.max)
-            nc.vector.tensor_tensor(e[:], e[:], cap[:, of_half], ALU.min)
             e_max = halves.tile([P, T], F32, name="e_max")
             nc.vector.tensor_reduce(e_max[:], e[:], axis=X, op=ALU.max)
             nc.vector.tensor_tensor(e[:], e[:], e_max[:].unsqueeze(2).to_broadcast(small), ALU.subtract)
-            att.append(halves.tile(small, F32, name="att"))
             nc.scalar.activation(att[h][:], e[:], ACT.Exp)
-            att_sum = halves.tile([P, T], F32, name="att_sum")
-            nc.vector.tensor_reduce(att_sum[:], att[h][:], axis=X, op=ALU.add)
-            nc.vector.reciprocal(att_sum[:], att_sum[:])
-            nc.vector.tensor_tensor(att[h][:], att[h][:], att_sum[:].unsqueeze(2).to_broadcast(small), ALU.mult)
+            nc.vector.tensor_reduce(inv_sum[h][:], att[h][:], axis=X, op=ALU.add)
+            nc.vector.reciprocal(inv_sum[h][:], inv_sum[h][:])
 
-        whT = []
-        for g in range(NGROUP):
-            whT.append(groups.tile([CHUNK, CPG, M], F32, name="whT"))
+        whT = [groups.tile([CHUNK, CPG, M], F32, name="whT") for g in range(NGROUP)]
+
+        def transpose_group(g):
             for pair in range(CPG // 2):
                 whT_ps = banks.tile([CHUNK, 2, M], F32, name="whT_ps", tag="bank")
                 for k in range(2):
@@ -137,26 +132,32 @@ def tile_numbergraphencoder_kernel(tc, table, w, a_src, a_dst, adj, offs, out):
                 nc.scalar.activation(whT[g][:, 2 * pair : 2 * pair + 2, :], whT_ps[:], ACT.Copy)
 
         wide = [P, T, GRAPHS, T]
-        attT = []
-        for h in range(HALVES):
+        attT = [halves.tile([CHUNK, PAIRS, CPH, GRAPHS, 2], F32, name="attT") for h in range(HALVES)]
+
+        def matrices(h):
             att_wide = halves.tile(wide, F32, name="att_wide")
             nc.vector.tensor_tensor(
                 att_wide[:],
                 att[h][:].unsqueeze(2).to_broadcast(wide),
-                graph_onehot[:].unsqueeze(1).unsqueeze(3).to_broadcast(wide),
+                inv_sum[h][:].unsqueeze(2).unsqueeze(3).to_broadcast(wide),
                 ALU.mult,
             )
-            attT.append(halves.tile([CHUNK, PAIRS, P, 2], F32, name="attT"))
             for a in range(PAIRS):
                 attT_ps = banks.tile([CHUNK, P, 2], F32, name="attT_ps", tag="bank")
                 for l in range(2):
                     nc.tensor.transpose(
                         attT_ps[:, :, l], att_wide[:, 2 * a + l].rearrange("q g t -> q (g t)"), ident[:]
                     )
-                nc.vector.tensor_copy(attT[h][:, a], attT_ps[:])
+                nc.vector.tensor_tensor(
+                    attT[h][:, a],
+                    attT_ps[:].rearrange("p (c g) l -> p c g l", g=GRAPHS),
+                    own_graph[:].unsqueeze(1).unsqueeze(3).to_broadcast([CHUNK, CPH, GRAPHS, 2]),
+                    ALU.mult,
+                )
 
         out_block = out.rearrange("(m b) j -> b m j", b=BLOCKS)
-        for g in range(NGROUP):
+
+        def products(g):
             for b in range(BLOCKS):
                 out_ps = banks.tile([P, PAIRS, CPG * GRAPHS, 2], F32, name="out_ps", tag="bank")
                 for k in range(CPG):
@@ -164,7 +165,7 @@ def tile_numbergraphencoder_kernel(tc, table, w, a_src, a_dst, adj, offs, out):
                     nc.tensor.matmul(
                         out_ps[:, :, k * GRAPHS : (k + 1) * GRAPHS, :],
                         whT[g][:, k, b * P : (b + 1) * P],
-                        attT[h][:, :, c * GRAPHS : (c + 1) * GRAPHS, :],
+                        attT[h][:, :, c],
                         start=True,
                         stop=True,
                     )
@@ -173,3 +174,14 @@ def tile_numbergraphencoder_kernel(tc, table, w, a_src, a_dst, adj, offs, out):
                 nc.sync.dma_start(
                     out_block[b, :, g * GROUP : (g + 1) * GROUP], out_sb[:].rearrange("m q a l -> m (q a l)")
                 )
+
+        for h in range(HALVES):
+            softmax(h)
+        for g in range(NGROUP - 1):
+            transpose_group(g)
+        matrices(0)
+        transpose_group(NGROUP - 1)
+        products(0)
+        matrices(1)
+        for g in range(1, NGROUP):
+            products(g)

@@ -14,13 +14,12 @@ T = 6
 BLOCKS = M // P
 BANK = 512
 HALVES = N // T // P
-CHUNK = 96
-GRAPHS = CHUNK // T
-CPH = P // GRAPHS
 PIECE = BANK
-GROUP = 384
-CPG = GROUP // CHUNK
-NGROUP = N // GROUP
+Q = N // T
+GRAPHS = P // T
+CHUNK = GRAPHS * T
+CPG = 2
+NGROUP = -(-N // (CPG * CHUNK))
 PAIRS = T // 2
 WARM = 8
 NEG_SLOPE = 0.2
@@ -65,15 +64,18 @@ def tile_numbergraphencoder_kernel(tc, table, w, a_src, a_dst, adj, offs, out):
         ident = held.tile([P, P], F32, name="ident")
         make_identity(nc, ident[:])
         cap = held.tile([P, HALVES * T, T], F32, name="cap")
-        nc.vector.tensor_scalar(cap[:], adj_sb[:], HUGE, MASK_VAL / NEG_SLOPE, ALU.mult, ALU.add)
-        own_graph = held.tile([CHUNK, GRAPHS], F32, name="own_graph")
+        nc.vector.tensor_scalar(cap[:], adj_sb[:], HUGE, MASK_VAL, ALU.mult, ALU.add)
+        own_graph = held.tile([CHUNK, Q], F32, name="own_graph")
         nc.gpsimd.memset(own_graph[:], 1.0)
-        nc.gpsimd.affine_select(
-            own_graph[:], own_graph[:], [[-T, GRAPHS]], ALU.is_ge, 0.0, base=0, channel_multiplier=1
-        )
-        nc.gpsimd.affine_select(
-            own_graph[:], own_graph[:], [[T, GRAPHS]], ALU.is_ge, 0.0, base=T - 1, channel_multiplier=-1
-        )
+        whole = Q // GRAPHS * GRAPHS
+        for part, pattern in ((own_graph[:, :whole], [whole // GRAPHS, GRAPHS]), (own_graph[:, whole:], [1, Q - whole])):
+            chunks, graphs_of_chunk = pattern
+            nc.gpsimd.affine_select(
+                part, part, [[0, chunks], [-T, graphs_of_chunk]], ALU.is_ge, 0.0, base=0, channel_multiplier=1
+            )
+            nc.gpsimd.affine_select(
+                part, part, [[0, chunks], [T, graphs_of_chunk]], ALU.is_ge, 0.0, base=T - 1, channel_multiplier=-1
+            )
 
         w_block = w_sb[:].rearrange("k (m b) -> k b m", b=BLOCKS)
         wh_bf = held.tile([P, BLOCKS, N], BF16, name="wh_bf")
@@ -91,26 +93,30 @@ def tile_numbergraphencoder_kernel(tc, table, w, a_src, a_dst, adj, offs, out):
                     nc.vector.tensor_copy(wh_bf[:, b, cols], wh_ps[:])
                     nc.vector.tensor_copy(wh_f32[:, b, cols], wh_ps[:])
 
+        by_node = wh_bf[:].rearrange("m b (q i) -> m b i q", i=T)
         small = [P, T, T]
         att = [halves.tile(small, F32, name="att") for h in range(HALVES)]
         inv_sum = [halves.tile([P, T], F32, name="inv_sum") for h in range(HALVES)]
 
-        by_node = wh_bf[:].rearrange("m b (q n) -> m b n q", n=T)
-
         def softmax(h):
-            of_half = slice(h * P, (h + 1) * P)
-            e_ps = small_ps.tile(small, F32, name="e_ps", tag="small")
-            for b in reversed(range(BLOCKS)):
-                a_row, a_col = (a_cols[:, s, b : b + 1].to_broadcast([P, T]) for s in range(2))
-                for n in range(T):
-                    first = b == BLOCKS - 1 and n == 0
-                    nc.tensor.matmul(e_ps[:, n], by_node[:, b, n, of_half], a_row, start=first, stop=False)
-                for n in range(T):
-                    last = b == 0 and n == T - 1
-                    nc.tensor.matmul(e_ps[:, :, n], by_node[:, b, n, of_half], a_col, start=False, stop=last)
+            sd_ps = small_ps.tile([P, T, 2], F32, name="sd_ps", tag="small")
+            for i in range(T):
+                for b in range(BLOCKS):
+                    nc.tensor.matmul(
+                        sd_ps[:, i],
+                        by_node[:, b, i, h * P : (h + 1) * P],
+                        a_cols[:, :, b],
+                        start=(b == 0),
+                        stop=(b == BLOCKS - 1),
+                    )
+            sd = halves.tile([P, T, 2], F32, name="sd")
+            nc.vector.tensor_copy(sd[:], sd_ps[:])
             e = halves.tile(small, F32, name="e")
-            nc.vector.tensor_tensor(e[:], e_ps[:], cap[:, h * T : (h + 1) * T], ALU.min)
+            nc.vector.tensor_tensor(
+                e[:], sd[:, :, 0:1].to_broadcast(small), sd[:, :, 1].unsqueeze(1).to_broadcast(small), ALU.add
+            )
             nc.vector.scalar_tensor_tensor(e[:], e[:], NEG_SLOPE, e[:], ALU.mult, ALU.max)
+            nc.vector.tensor_tensor(e[:], e[:], cap[:, h * T : (h + 1) * T], ALU.min)
             e_max = halves.tile([P, T], F32, name="e_max")
             nc.vector.tensor_reduce(e_max[:], e[:], axis=X, op=ALU.max)
             nc.vector.tensor_tensor(e[:], e[:], e_max[:].unsqueeze(2).to_broadcast(small), ALU.subtract)
@@ -118,31 +124,35 @@ def tile_numbergraphencoder_kernel(tc, table, w, a_src, a_dst, adj, offs, out):
             nc.vector.tensor_reduce(inv_sum[h][:], att[h][:], axis=X, op=ALU.add)
             nc.vector.reciprocal(inv_sum[h][:], inv_sum[h][:])
 
+        def chunks_of(g):
+            return [(k, c, min(CHUNK, N - c * CHUNK)) for k, c in enumerate(range(g * CPG, (g + 1) * CPG)) if c * CHUNK < N]
+
         whT = [groups.tile([CHUNK, CPG, M], F32, name="whT") for g in range(NGROUP)]
 
         def transpose_group(g):
-            for pair in range(CPG // 2):
-                whT_ps = banks.tile([CHUNK, 2, M], F32, name="whT_ps", tag="bank")
-                for k in range(2):
-                    first = g * GROUP + (2 * pair + k) * CHUNK
-                    for b in range(BLOCKS):
-                        nc.tensor.transpose(
-                            whT_ps[:, k, b * P : (b + 1) * P], wh_f32[:, b, first : first + CHUNK], ident[:]
-                        )
-                nc.scalar.activation(whT[g][:, 2 * pair : 2 * pair + 2, :], whT_ps[:], ACT.Copy)
+            whT_ps = banks.tile([CHUNK, CPG, M], F32, name="whT_ps", tag="bank")
+            chunks = chunks_of(g)
+            for k, c, rows in chunks:
+                for b in range(BLOCKS):
+                    nc.tensor.transpose(
+                        whT_ps[:rows, k, b * P : (b + 1) * P], wh_f32[:, b, c * CHUNK : c * CHUNK + rows], ident[:]
+                    )
+            filled = slice(0, chunks[0][2]), slice(0, len(chunks))
+            nc.scalar.activation(whT[g][filled], whT_ps[filled], ACT.Copy)
 
-        wide = [P, T, GRAPHS, T]
-        attT = [halves.tile([CHUNK, PAIRS, CPH, GRAPHS, 2], F32, name="attT") for h in range(HALVES)]
+        wide = [P, 2, GRAPHS, T]
+        attT = [halves.tile([CHUNK, PAIRS, P, 2], F32, name="attT") for h in range(HALVES)]
 
-        def matrices(h):
-            att_wide = halves.tile(wide, F32, name="att_wide")
-            nc.vector.tensor_tensor(
-                att_wide[:],
-                att[h][:].unsqueeze(2).to_broadcast(wide),
-                inv_sum[h][:].unsqueeze(2).unsqueeze(3).to_broadcast(wide),
-                ALU.mult,
-            )
+        def matrices(h, widening_engine):
+            att_wide = halves.tile([P, T, GRAPHS, T], F32, name="att_wide")
             for a in range(PAIRS):
+                pair = slice(2 * a, 2 * a + 2)
+                widening_engine.tensor_tensor(
+                    att_wide[:, pair],
+                    att[h][:, pair].unsqueeze(2).to_broadcast(wide),
+                    inv_sum[h][:, pair].unsqueeze(2).unsqueeze(3).to_broadcast(wide),
+                    ALU.mult,
+                )
                 attT_ps = banks.tile([CHUNK, P, 2], F32, name="attT_ps", tag="bank")
                 for l in range(2):
                     nc.tensor.transpose(
@@ -150,38 +160,46 @@ def tile_numbergraphencoder_kernel(tc, table, w, a_src, a_dst, adj, offs, out):
                     )
                 nc.vector.tensor_tensor(
                     attT[h][:, a],
-                    attT_ps[:].rearrange("p (c g) l -> p c g l", g=GRAPHS),
-                    own_graph[:].unsqueeze(1).unsqueeze(3).to_broadcast([CHUNK, CPH, GRAPHS, 2]),
+                    attT_ps[:],
+                    own_graph[:, h * P : (h + 1) * P].unsqueeze(2).to_broadcast([CHUNK, P, 2]),
                     ALU.mult,
                 )
 
         out_block = out.rearrange("(m b) j -> b m j", b=BLOCKS)
 
         def products(g):
+            chunks = chunks_of(g)
+            first_graph = g * CPG * GRAPHS
+            graphs_of_group = sum(rows for k, c, rows in chunks) // T
             for b in range(BLOCKS):
-                out_ps = banks.tile([P, PAIRS, CPG * GRAPHS, 2], F32, name="out_ps", tag="bank")
-                for k in range(CPG):
-                    h, c = divmod(g * CPG + k, CPH)
-                    nc.tensor.matmul(
-                        out_ps[:, :, k * GRAPHS : (k + 1) * GRAPHS, :],
-                        whT[g][:, k, b * P : (b + 1) * P],
-                        attT[h][:, :, c],
-                        start=True,
-                        stop=True,
-                    )
-                out_sb = stage.tile([P, CPG * GRAPHS, PAIRS, 2], F32, name="out_sb")
+                out_ps = banks.tile([P, PAIRS, graphs_of_group, 2], F32, name="out_ps", tag="bank")
+                for k, c, rows in chunks:
+                    for h in range(HALVES):
+                        start = max(c * GRAPHS, h * P)
+                        end = min(c * GRAPHS + rows // T, (h + 1) * P)
+                        if start < end:
+                            nc.tensor.matmul(
+                                out_ps[:, :, start - first_graph : end - first_graph, :],
+                                whT[g][:rows, k, b * P : (b + 1) * P],
+                                attT[h][:rows, :, start - h * P : end - h * P],
+                                start=True,
+                                stop=True,
+                            )
+                out_sb = stage.tile([P, graphs_of_group, PAIRS, 2], F32, name="out_sb")
                 nc.scalar.activation(out_sb[:], out_ps[:].rearrange("m a q l -> m q a l"), ACT.Relu)
                 nc.sync.dma_start(
-                    out_block[b, :, g * GROUP : (g + 1) * GROUP], out_sb[:].rearrange("m q a l -> m (q a l)")
+                    out_block[b, :, first_graph * T : (first_graph + graphs_of_group) * T],
+                    out_sb[:].rearrange("m q a l -> m (q a l)"),
                 )
 
         for h in range(HALVES):
             softmax(h)
-        for g in range(NGROUP - 1):
+        for g in range(NGROUP - 2):
             transpose_group(g)
-        matrices(0)
-        transpose_group(NGROUP - 1)
+        matrices(0, nc.vector)
+        for g in range(NGROUP - 2, NGROUP):
+            transpose_group(g)
         products(0)
-        matrices(1)
+        matrices(1, nc.gpsimd)
         for g in range(1, NGROUP):
             products(g)

@@ -21,7 +21,7 @@ CHUNK = GRAPHS * T
 CPG = 2
 NGROUP = -(-N // (CPG * CHUNK))
 PAIRS = T // 2
-WARM = 8
+WARM = 4
 NEG_SLOPE = 0.2
 MASK_VAL = -1e9
 HUGE = 3e38
@@ -88,9 +88,11 @@ def tile_numbergraphencoder_kernel(tc, table, w, a_src, a_dst, adj, offs, out):
                 nc.tensor.matmul(wh_ps[:], w_block[:, b], table_sb[:].indirect(piece), start=True, stop=True)
                 if b == 0:
                     nc.scalar.activation(wh_bf[:, b, cols], wh_ps[:], ACT.Copy)
-                    nc.scalar.activation(wh_f32[:, b, cols], wh_ps[:], ACT.Copy)
                 else:
                     nc.vector.tensor_copy(wh_bf[:, b, cols], wh_ps[:])
+                if b == 0 or i == N // PIECE - 1:
+                    nc.scalar.activation(wh_f32[:, b, cols], wh_ps[:], ACT.Copy)
+                else:
                     nc.vector.tensor_copy(wh_f32[:, b, cols], wh_ps[:])
 
         by_node = wh_bf[:].rearrange("m b (q i) -> m b i q", i=T)

@@ -64,7 +64,7 @@ def tile_numbergraphencoder_kernel(tc, table, w, a_src, a_dst, adj, offs, out):
         ident = held.tile([P, P], F32, name="ident")
         make_identity(nc, ident[:])
         cap = held.tile([P, HALVES * T, T], F32, name="cap")
-        nc.vector.tensor_scalar(cap[:], adj_sb[:], HUGE, MASK_VAL, ALU.mult, ALU.add)
+        nc.vector.tensor_scalar(cap[:], adj_sb[:], HUGE, MASK_VAL / NEG_SLOPE, ALU.mult, ALU.add)
         own_graph = held.tile([CHUNK, Q], F32, name="own_graph")
         nc.gpsimd.memset(own_graph[:], 1.0)
         whole = Q // GRAPHS * GRAPHS
@@ -111,20 +111,20 @@ def tile_numbergraphencoder_kernel(tc, table, w, a_src, a_dst, adj, offs, out):
                         start=(b == 0),
                         stop=(b == BLOCKS - 1),
                     )
-            sd = halves.tile([P, T, 2], F32, name="sd")
-            nc.vector.tensor_copy(sd[:], sd_ps[:])
             e = halves.tile(small, F32, name="e")
-            nc.vector.tensor_tensor(
-                e[:], sd[:, :, 0:1].to_broadcast(small), sd[:, :, 1].unsqueeze(1).to_broadcast(small), ALU.add
-            )
+            for i in range(T):
+                nc.vector.scalar_tensor_tensor(
+                    e[:, i], sd_ps[:, :, 1], sd_ps[:, i, 0:1], cap[:, h * T + i], ALU.add, ALU.min
+                )
             nc.vector.scalar_tensor_tensor(e[:], e[:], NEG_SLOPE, e[:], ALU.mult, ALU.max)
-            nc.vector.tensor_tensor(e[:], e[:], cap[:, h * T : (h + 1) * T], ALU.min)
-            e_max = halves.tile([P, T], F32, name="e_max")
-            nc.vector.tensor_reduce(e_max[:], e[:], axis=X, op=ALU.max)
-            nc.vector.tensor_tensor(e[:], e[:], e_max[:].unsqueeze(2).to_broadcast(small), ALU.subtract)
-            nc.scalar.activation(att[h][:], e[:], ACT.Exp)
-            nc.vector.tensor_reduce(inv_sum[h][:], att[h][:], axis=X, op=ALU.add)
-            nc.vector.reciprocal(inv_sum[h][:], inv_sum[h][:])
+            minus_max = halves.tile([P, T], F32, name="minus_max")
+            nc.vector.tensor_reduce(minus_max[:], e[:], axis=X, op=ALU.max, negate=True)
+            att_sum = halves.tile([P, T], F32, name="att_sum")
+            for i in range(T):
+                nc.scalar.activation(
+                    att[h][:, i], e[:, i], ACT.Exp, bias=minus_max[:, i : i + 1], accum_out=att_sum[:, i : i + 1]
+                )
+            nc.vector.reciprocal(inv_sum[h][:], att_sum[:])
 
         def chunks_of(g):
             return [(k, c, min(CHUNK, N - c * CHUNK)) for k, c in enumerate(range(g * CPG, (g + 1) * CPG)) if c * CHUNK < N]

import concourse.mybir as mybir
from concourse.masks import make_identity

BF16, F32, U16 = mybir.dt.bfloat16, mybir.dt.float32, mybir.dt.uint16
ALU = mybir.AluOpType
ACT = mybir.ActivationFunctionType
X = mybir.AxisListType.X

P = 128
S = 2048
M = 256
N = 1536
T = 6
BLOCKS = M // P
BANK = 512
HALVES = N // T // P
PIECE = BANK
Q = N // T
GRAPHS = P // T
CHUNK = GRAPHS * T
CPG = 2
NGROUP = -(-N // (CPG * CHUNK))
PAIRS = T // 2
WARM = 4
NEG_SLOPE = 0.2
MASK_VAL = -1e9
HUGE = 3e38
A_STEP = 16

FLOPS = 2 * N * M * (P + 2 + T)


def tile_numbergraphencoder_kernel(tc, table, w, a_src, a_dst, adj, offs, out):
    nc = tc.nc
    with (
        tc.tile_pool(name="held", bufs=1) as held,
        tc.tile_pool(name="halves", bufs=HALVES) as halves,
        tc.tile_pool(name="groups", bufs=NGROUP) as groups,
        tc.tile_pool(name="stage", bufs=NGROUP * BLOCKS) as stage,
        tc.psum_pool(name="banks", bufs=6) as banks,
        tc.psum_pool(name="small_ps", bufs=2) as small_ps,
    ):
        offsets = held.tile([P, N // 16], U16, name="offsets")
        nc.sync.dma_start(offsets[:], offs)
        table_sb = held.tile([P, S], BF16, name="table_sb")
        nc.sync.dma_start(table_sb[:], table)
        w_sb = held.tile([P, M], BF16, name="w_sb")
        nc.scalar.dma_start(w_sb[:], w)
        a_cols = held.tile([P, 2, A_STEP], BF16, name="a_cols")
        nc.scalar.dma_start(a_cols[:, 0, 0:BLOCKS], a_src.rearrange("(m b) o -> m (b o)", b=BLOCKS))
        nc.scalar.dma_start(a_cols[:, 1, 0:BLOCKS], a_dst.rearrange("(m b) o -> m (b o)", b=BLOCKS))
        adj_sb = held.tile([P, HALVES * T, T], F32, name="adj_sb")
        nc.sync.dma_start(
            adj_sb[:].rearrange("q (h i) t -> q h (i t)", h=HALVES),
            adj.rearrange("(h q i) t -> q h (i t)", h=HALVES, i=T),
        )

        zeros = held.tile([P, BANK], BF16, name="zeros")
        nc.vector.memset(zeros[:], 0.0)
        warm_ps = small_ps.tile([P, BANK], F32, name="warm_ps", tag="small")
        for i in range(WARM):
            nc.tensor.matmul(warm_ps[:], zeros[:, :P], zeros[:], start=True, stop=True)

        ident = held.tile([P, P], F32, name="ident")
        make_identity(nc, ident[:])
        cap = held.tile([P, HALVES * T, T], F32, name="cap")
        nc.vector.tensor_scalar(cap[:], adj_sb[:], HUGE, MASK_VAL / NEG_SLOPE, ALU.mult, ALU.add)
        own_graph = held.tile([CHUNK, Q], F32, name="own_graph")
        nc.gpsimd.memset(own_graph[:], 1.0)
        whole = Q // GRAPHS * GRAPHS
        for part, pattern in ((own_graph[:, :whole], [whole // GRAPHS, GRAPHS]), (own_graph[:, whole:], [1, Q - whole])):
            chunks, graphs_of_chunk = pattern
            nc.gpsimd.affine_select(
                part, part, [[0, chunks], [-T, graphs_of_chunk]], ALU.is_ge, 0.0, base=0, channel_multiplier=1
            )
            nc.gpsimd.affine_select(
                part, part, [[0, chunks], [T, graphs_of_chunk]], ALU.is_ge, 0.0, base=T - 1, channel_multiplier=-1
            )

        w_block = w_sb[:].rearrange("k (m b) -> k b m", b=BLOCKS)
        wh_bf = held.tile([P, BLOCKS, N], BF16, name="wh_bf")
        wh_f32 = held.tile([P, BLOCKS, N], F32, name="wh_f32")
        for i in range(N // PIECE):
            cols = slice(i * PIECE, (i + 1) * PIECE)
            piece = offsets[:, i * PIECE // 16 : (i + 1) * PIECE // 16]
            for b in range(BLOCKS):
                wh_ps = banks.tile([P, PIECE], F32, name="wh_ps", tag="bank")
                nc.tensor.matmul(wh_ps[:], w_block[:, b], table_sb[:].indirect(piece), start=True, stop=True)
                if b == 0:
                    nc.scalar.activation(wh_bf[:, b, cols], wh_ps[:], ACT.Copy)
                else:
                    nc.vector.tensor_copy(wh_bf[:, b, cols], wh_ps[:])
                if b == 0 or i == N // PIECE - 1:
                    nc.scalar.activation(wh_f32[:, b, cols], wh_ps[:], ACT.Copy)
                else:
                    nc.vector.tensor_copy(wh_f32[:, b, cols], wh_ps[:])

        by_node = wh_bf[:].rearrange("m b (q i) -> m b i q", i=T)
        small = [P, T, T]
        att = [halves.tile(small, F32, name="att") for h in range(HALVES)]
        inv_sum = [halves.tile([P, T], F32, name="inv_sum") for h in range(HALVES)]

        def softmax(h):
            sd_ps = small_ps.tile([P, T, 2], F32, name="sd_ps", tag="small")
            for i in range(T):
                for b in range(BLOCKS):
                    nc.tensor.matmul(
                        sd_ps[:, i],
                        by_node[:, b, i, h * P : (h + 1) * P],
                        a_cols[:, :, b],
                        start=(b == 0),
                        stop=(b == BLOCKS - 1),
                    )
            e = halves.tile(small, F32, name="e")
            for i in range(T):
                nc.vector.scalar_tensor_tensor(
                    e[:, i], sd_ps[:, :, 1], sd_ps[:, i, 0:1], cap[:, h * T + i], ALU.add, ALU.min
                )
            nc.vector.scalar_tensor_tensor(e[:], e[:], NEG_SLOPE, e[:], ALU.mult, ALU.max)
            minus_max = halves.tile([P, T], F32, name="minus_max")
            nc.vector.tensor_reduce(minus_max[:], e[:], axis=X, op=ALU.max, negate=True)
            att_sum = halves.tile([P, T], F32, name="att_sum")
            for i in range(T):
                nc.scalar.activation(
                    att[h][:, i], e[:, i], ACT.Exp, bias=minus_max[:, i : i + 1], accum_out=att_sum[:, i : i + 1]
                )
            nc.vector.reciprocal(inv_sum[h][:], att_sum[:])

        def chunks_of(g):
            return [(k, c, min(CHUNK, N - c * CHUNK)) for k, c in enumerate(range(g * CPG, (g + 1) * CPG)) if c * CHUNK < N]

        whT = [groups.tile([CHUNK, CPG, M], F32, name="whT") for g in range(NGROUP)]

        def transpose_group(g):
            whT_ps = banks.tile([CHUNK, CPG, M], F32, name="whT_ps", tag="bank")
            chunks = chunks_of(g)
            for k, c, rows in chunks:
                for b in range(BLOCKS):
                    nc.tensor.transpose(
                        whT_ps[:rows, k, b * P : (b + 1) * P], wh_f32[:, b, c * CHUNK : c * CHUNK + rows], ident[:]
                    )
            filled = slice(0, chunks[0][2]), slice(0, len(chunks))
            nc.scalar.activation(whT[g][filled], whT_ps[filled], ACT.Copy)

        wide = [P, 2, GRAPHS, T]
        attT = [halves.tile([CHUNK, PAIRS, P, 2], F32, name="attT") for h in range(HALVES)]

        def matrices(h, widening_engine):
            att_wide = halves.tile([P, T, GRAPHS, T], F32, name="att_wide")
            for a in range(PAIRS):
                pair = slice(2 * a, 2 * a + 2)
                widening_engine.tensor_tensor(
                    att_wide[:, pair],
                    att[h][:, pair].unsqueeze(2).to_broadcast(wide),
                    inv_sum[h][:, pair].unsqueeze(2).unsqueeze(3).to_broadcast(wide),
                    ALU.mult,
                )
                attT_ps = banks.tile([CHUNK, P, 2], F32, name="attT_ps", tag="bank")
                for l in range(2):
                    nc.tensor.transpose(
                        attT_ps[:, :, l], att_wide[:, 2 * a + l].rearrange("q g t -> q (g t)"), ident[:]
                    )
                nc.vector.tensor_tensor(
                    attT[h][:, a],
                    attT_ps[:],
                    own_graph[:, h * P : (h + 1) * P].unsqueeze(2).to_broadcast([CHUNK, P, 2]),
                    ALU.mult,
                )

        out_block = out.rearrange("(m b) j -> b m j", b=BLOCKS)

        def products(g):
            chunks = chunks_of(g)
            first_graph = g * CPG * GRAPHS
            graphs_of_group = sum(rows for k, c, rows in chunks) // T
            for b in range(BLOCKS):
                out_ps = banks.tile([P, PAIRS, graphs_of_group, 2], F32, name="out_ps", tag="bank")
                for k, c, rows in chunks:
                    for h in range(HALVES):
                        start = max(c * GRAPHS, h * P)
                        end = min(c * GRAPHS + rows // T, (h + 1) * P)
                        if start < end:
                            nc.tensor.matmul(
                                out_ps[:, :, start - first_graph : end - first_graph, :],
                                whT[g][:rows, k, b * P : (b + 1) * P],
                                attT[h][:rows, :, start - h * P : end - h * P],
                                start=True,
                                stop=True,
                            )
                out_sb = stage.tile([P, graphs_of_group, PAIRS, 2], F32, name="out_sb")
                nc.scalar.activation(out_sb[:], out_ps[:].rearrange("m a q l -> m q a l"), ACT.Relu)
                nc.sync.dma_start(
                    out_block[b, :, first_graph * T : (first_graph + graphs_of_group) * T],
                    out_sb[:].rearrange("m q a l -> m (q a l)"),
                )

        for h in range(HALVES):
            softmax(h)
        for g in range(NGROUP - 2):
            transpose_group(g)
        matrices(0, nc.vector)
        for g in range(NGROUP - 2, NGROUP):
            transpose_group(g)
        products(0)
        matrices(1, nc.gpsimd)
        for g in range(1, NGROUP):
            products(g)
